import numpy as np
import ml_dtypes


def mxq(x, axis, fmt="e4m3"):
    dtype, down = {"e4m3": (ml_dtypes.float8_e4m3fn, 7), "e5m2": (ml_dtypes.float8_e5m2, 14)}[fmt]
    v = np.moveaxis(np.asarray(x, np.float32).astype(ml_dtypes.bfloat16).astype(np.float64), axis, -1)
    blocks = v.reshape(v.shape[:-1] + (-1, 32))
    amax = np.abs(blocks).max(-1, keepdims=True)
    byte = np.maximum(np.where(amax > 0, np.frexp(amax)[1] - 1 + 127, 0) - down, 1)
    scale = np.exp2(byte - 127.0)
    codes = (blocks / scale).astype(np.float32).astype(dtype).astype(np.float64)
    return np.moveaxis((codes * scale).reshape(v.shape), -1, axis)


WIDE = False


def mx_kscale(k):
    if not WIDE:
        return np.ones(k)
    levels = np.array([20, -20, 10, -10, 0])
    a = np.random.permutation(np.resize(levels, k // 512 * 4)).reshape(k // 512, 4)
    idx = np.arange(k)
    return np.exp2(a[idx // 512, idx % 128 // 32])


BF16 = ml_dtypes.bfloat16


def bf(x):
    return np.asarray(x, np.float32).astype(BF16)


def f64(x):
    return np.asarray(x).astype(np.float64)


B, C, H, W = 2, 1024, 32, 32
P = H * W
GAMMA_INIT = 0.1


def setup_inputs():
    u = mx_kscale(C)
    gain = np.exp(0.5 * np.random.standard_normal((B, 1, H, W)))
    x0 = bf(np.random.standard_normal((B, C, H, W)) * gain)
    gamma0 = bf(GAMMA_INIT * np.eye(C) + np.abs(np.random.standard_normal((C, C))) / C)
    beta = bf(0.5 + np.random.random(C))
    g = bf(np.random.standard_normal((B, C, H, W)) * np.exp2(np.random.randint(-12, 1, (B, 1, H, W))) * 16.0)
    xf = f64(x0)
    norm = (f64(gamma0) @ (xf * xf).reshape(B, C, P)).reshape(B, C, H, W) + f64(beta)[None, :, None, None]
    y = xf / np.sqrt(norm)
    x = bf(xf * u[None, :, None, None])
    gamma = bf(f64(gamma0) / u[:, None])
    return {"x": x, "gamma": gamma, "beta": beta, "norm": np.asarray(norm, np.float32), "y": np.asarray(y, np.float32), "grad_out": g}


def reference(x, gamma, beta, norm, y, grad_out):
    g = f64(grad_out).reshape(B, C, P)
    xf = f64(x).reshape(B, C, P)
    n = f64(norm).reshape(B, C, P)
    yf = f64(y).reshape(B, C, P)
    rt = np.sqrt(n)
    dn = -0.5 * g * xf / (n * rt)
    m = mxq(f64(gamma), 0, "e4m3").T @ mxq(dn, 1, "e5m2")
    res = g / rt + 2.0 * yf * rt * m
    return res.reshape(B, C, H, W)

@@ -1,0 +1,165 @@
+from contextlib import ExitStack
+
+import concourse.mybir as mybir
+
+F32 = mybir.dt.float32
+BF16 = mybir.dt.bfloat16
+U32 = mybir.dt.uint32
+U8 = mybir.dt.uint8
+E4M3_X4 = mybir.dt.float8_e4m3fn_x4
+E5M2_X4 = mybir.dt.float8_e5m2_x4
+ACT = mybir.ActivationFunctionType
+ALU = mybir.AluOpType
+
+BATCH = 2
+CHANNELS = 1024
+PIXELS = 32 * 32
+P = 128
+PACK = 4
+K_PASS = P * PACK
+PASSES = CHANNELS // K_PASS
+N_TILE = 512
+BLOCKS = BATCH * PIXELS // N_TILE
+UNITS = BLOCKS * PASSES
+LAG = 2
+AHEAD = 2
+HALVES = (slice(0, PACK // 2), slice(PACK // 2, PACK))
+
+FLOPS = 2 * BATCH * PIXELS * CHANNELS * CHANNELS
+
+
+def regroup(nc, grouped, rows):
+    nc.scalar.copy(
+        out=grouped.rearrange("p (c i) t -> p c t i", i=4),
+        in_=rows.rearrange("p t (c i) -> p c t i", i=4),
+    )
+
+
+def tile_gdn_t_v_kernel(tc, x, gamma, beta, norm, y, grad_out, out):
+    nc = tc.nc
+
+    def units_of(ap):
+        return ap.rearrange("b (g t p) h w -> b g p t (h w)", t=PACK, p=P)
+
+    x_units = units_of(x)
+    norm_units = units_of(norm)
+    y_units = units_of(y)
+    grad_units = units_of(grad_out)
+    out_units = units_of(out)
+    gamma_passes = gamma.rearrange("(g t p) c -> g p t c", t=PACK, p=P)
+
+    def dram_unit(units, u):
+        block, g = divmod(u, PASSES)
+        b, part = divmod(block, PIXELS // N_TILE)
+        return units[b, g, :, :, part * N_TILE : (part + 1) * N_TILE]
+
+    with ExitStack() as stack:
+        keep = stack.enter_context(tc.tile_pool(name="keep", bufs=1))
+        stage = stack.enter_context(tc.tile_pool(name="stage", bufs=1))
+        loads = stack.enter_context(tc.tile_pool(name="loads", bufs=3))
+        short = stack.enter_context(tc.tile_pool(name="short", bufs=2))
+        saved = stack.enter_context(tc.tile_pool(name="saved", bufs=LAG + 2))
+        coded = stack.enter_context(tc.tile_pool(name="coded", bufs=LAG + 3))
+        psum = stack.enter_context(tc.psum_pool(name="psum", bufs=8))
+
+        gamma_codes = keep.tile([P, PASSES, CHANNELS], U32, align_bytes=64)
+        gamma_scales = keep.tile([P, PASSES, CHANNELS], U8, align_bytes=64)
+
+        inputs = {}
+        held = {}
+
+        def load_inputs(u):
+            norm_t = loads.tile([P, PACK, N_TILE], F32)
+            grad_t = loads.tile([P, PACK, N_TILE], BF16)
+            x_t = loads.tile([P, PACK, N_TILE], BF16)
+            for h in HALVES:
+                nc.sync.dma_start(out=norm_t[:, h, :], in_=dram_unit(norm_units, u)[:, h, :])
+                nc.sync.dma_start(out=grad_t[:, h, :], in_=dram_unit(grad_units, u)[:, h, :])
+                nc.sync.dma_start(out=x_t[:, h, :], in_=dram_unit(x_units, u)[:, h, :])
+            inputs[u] = (norm_t, grad_t, x_t)
+
+        def quantise_gamma():
+            for g in range(PASSES):
+                gamma_rows = stage.tile([P, PACK, CHANNELS], BF16)
+                nc.sync.dma_start(out=gamma_rows[:], in_=gamma_passes[g])
+                gamma_grouped = stage.tile([P, CHANNELS, PACK], BF16, align_bytes=64)
+                for c0 in range(0, CHANNELS, N_TILE):
+                    regroup(nc, gamma_grouped[:, c0 : c0 + N_TILE, :], gamma_rows[:, :, c0 : c0 + N_TILE])
+                nc.vector.quantize_mx(
+                    out=gamma_codes[:, g, :].bitcast(E4M3_X4),
+                    scales=gamma_scales[:, g, :],
+                    in_=gamma_grouped[:].rearrange("p c t -> p (c t)"),
+                )
+
+        def make_dn(u):
+            norm_t, grad_t, x_t = inputs[u]
+            inv_root = short.tile([P, PACK, N_TILE], F32)
+            inv_norm = saved.tile([P, PACK, N_TILE], F32)
+            for h in HALVES:
+                nc.scalar.activation(out=inv_root[:, h, :], in_=norm_t[:, h, :], func=ACT.Abs_reciprocal_sqrt)
+            for h in HALVES:
+                nc.scalar.activation(out=inv_norm[:, h, :], in_=inv_root[:, h, :], func=ACT.Square)
+            grad_over_norm = saved.tile([P, PACK, N_TILE], F32)
+            x_over_root = short.tile([P, PACK, N_TILE], F32)
+            dn = short.tile([P, PACK, N_TILE], BF16)
+            for h in HALVES:
+                nc.vector.tensor_tensor(out=grad_over_norm[:, h, :], in0=grad_t[:, h, :], in1=inv_norm[:, h, :], op=ALU.mult)
+            for h in HALVES:
+                nc.vector.tensor_tensor(out=x_over_root[:, h, :], in0=x_t[:, h, :], in1=inv_root[:, h, :], op=ALU.mult)
+            for h in HALVES:
+                nc.vector.scalar_tensor_tensor(
+                    out=dn[:, h, :], in0=grad_over_norm[:, h, :], scalar=-0.5, in1=x_over_root[:, h, :],
+                    op0=ALU.mult, op1=ALU.mult,
+                )
+            dn_grouped = short.tile([P, N_TILE, PACK], BF16, align_bytes=64)
+            regroup(nc, dn_grouped[:], dn[:])
+            dn_codes = coded.tile([P, N_TILE], U32, align_bytes=64)
+            dn_scales = coded.tile([P, N_TILE], U8, align_bytes=64)
+            nc.vector.quantize_mx(
+                out=dn_codes[:].bitcast(E5M2_X4),
+                scales=dn_scales[:],
+                in_=dn_grouped[:].rearrange("p w t -> p (w t)"),
+            )
+            held[u] = (inv_norm, grad_over_norm, dn_codes, dn_scales)
+
+        def finish(u):
+            block, g_out = divmod(u, PASSES)
+            inv_norm, grad_over_norm = held[u][0:2]
+            result = short.tile([P, PACK, N_TILE], F32)
+            nc.sync.dma_start(out=result[:], in_=dram_unit(y_units, u))
+            root = short.tile([P, PACK, N_TILE], F32)
+            for h in HALVES:
+                nc.scalar.activation(out=root[:, h, :], in_=inv_norm[:, h, :], func=ACT.Abs_reciprocal_sqrt)
+            for t in range(PACK):
+                c0 = (g_out * PACK + t) * P
+                m = psum.tile([P, N_TILE], F32)
+                for g in range(PASSES):
+                    dn_codes, dn_scales = held[block * PASSES + g][2:4]
+                    nc.tensor.matmul_mx(
+                        out=m[:],
+                        lhsT=gamma_codes[:, g, c0 : c0 + P].bitcast(E4M3_X4),
+                        lhsT_scale=gamma_scales[:, g, c0 : c0 + P],
+                        rhs=dn_codes[:].bitcast(E5M2_X4),
+                        rhs_scale=dn_scales[:],
+                        start=(g == 0),
+                        stop=(g == PASSES - 1),
+                    )
+                nc.vector.scalar_tensor_tensor(
+                    out=result[:, t, :], in0=m[:], scalar=2.0, in1=result[:, t, :], op0=ALU.mult, op1=ALU.mult,
+                )
+            for h in HALVES:
+                nc.vector.tensor_tensor(out=result[:, h, :], in0=result[:, h, :], in1=grad_over_norm[:, h, :], op=ALU.add)
+            for h in HALVES:
+                nc.vector.tensor_tensor(out=result[:, h, :], in0=result[:, h, :], in1=root[:, h, :], op=ALU.mult)
+                nc.sync.dma_start(out=dram_unit(out_units, u)[:, h, :], in_=result[:, h, :])
+
+        for u in range(AHEAD):
+            load_inputs(u)
+        quantise_gamma()
+        for i in range(UNITS + LAG):
+            if i + AHEAD < UNITS:
+                load_inputs(i + AHEAD)
+            if i < UNITS:
+                make_dn(i)
+            if i >= LAG:
+                finish(i - LAG)

@@ -104,8 +104,9 @@ def tile_gdn_t_v_kernel(tc, x, gamma, beta, norm, y, grad_out, out):
             dn = short.tile([P, PACK, N_TILE], BF16)
             for h in HALVES:
                 nc.vector.tensor_tensor(out=grad_over_norm[:, h, :], in0=grad_t[:, h, :], in1=inv_norm[:, h, :], op=ALU.mult)
-            for h in HALVES:
-                nc.vector.tensor_tensor(out=x_over_root[:, h, :], in0=x_t[:, h, :], in1=inv_root[:, h, :], op=ALU.mult)
+            helper = nc.gpsimd if u > LAG else nc.vector
+            nc.vector.tensor_tensor(out=x_over_root[:, HALVES[0], :], in0=x_t[:, HALVES[0], :], in1=inv_root[:, HALVES[0], :], op=ALU.mult)
+            helper.tensor_tensor(out=x_over_root[:, HALVES[1], :], in0=x_t[:, HALVES[1], :], in1=inv_root[:, HALVES[1], :], op=ALU.mult)
             for h in HALVES:
                 nc.vector.scalar_tensor_tensor(
                     out=dn[:, h, :], in0=grad_over_norm[:, h, :], scalar=-0.5, in1=x_over_root[:, h, :],

@@ -1,6 +1,7 @@
 from contextlib import ExitStack
 
 import concourse.mybir as mybir
+from concourse.masks import make_identity
 
 F32 = mybir.dt.float32
 BF16 = mybir.dt.bfloat16
@@ -28,11 +29,8 @@ HALVES = (slice(0, PACK // 2), slice(PACK // 2, PACK))
 FLOPS = 2 * BATCH * PIXELS * CHANNELS * CHANNELS
 
 
-def regroup(nc, grouped, rows):
-    nc.scalar.copy(
-        out=grouped.rearrange("p (c i) t -> p c t i", i=4),
-        in_=rows.rearrange("p t (c i) -> p c t i", i=4),
-    )
+def flat(ap):
+    return ap.rearrange("p t w -> p (t w)")
 
 
 def tile_gdn_t_v_kernel(tc, x, gamma, beta, norm, y, grad_out, out):
@@ -55,20 +53,28 @@ def tile_gdn_t_v_kernel(tc, x, gamma, beta, norm, y, grad_out, out):
 
     with ExitStack() as stack:
         keep = stack.enter_context(tc.tile_pool(name="keep", bufs=1))
-        stage = stack.enter_context(tc.tile_pool(name="stage", bufs=1))
+        stage = stack.enter_context(tc.tile_pool(name="stage", bufs=PASSES))
         loads = stack.enter_context(tc.tile_pool(name="loads", bufs=3))
         short = stack.enter_context(tc.tile_pool(name="short", bufs=2))
-        saved = stack.enter_context(tc.tile_pool(name="saved", bufs=LAG + 2))
+        once = stack.enter_context(tc.tile_pool(name="once", bufs=1))
+        kept = stack.enter_context(tc.tile_pool(name="kept", bufs=LAG + 2))
+        results = stack.enter_context(tc.tile_pool(name="results", bufs=LAG + 3))
         coded = stack.enter_context(tc.tile_pool(name="coded", bufs=LAG + 3))
-        psum = stack.enter_context(tc.psum_pool(name="psum", bufs=8))
+        psum_m = stack.enter_context(tc.psum_pool(name="psum_m", bufs=4))
+        psum_x = stack.enter_context(tc.psum_pool(name="psum_x", bufs=4))
 
         gamma_codes = keep.tile([P, PASSES, CHANNELS], U32, align_bytes=64)
         gamma_scales = keep.tile([P, PASSES, CHANNELS], U8, align_bytes=64)
+        identity = keep.tile([P, P], BF16)
+        make_identity(nc, identity[:])
 
-        inputs = {}
-        held = {}
+        raw = {}
+        roots = {}
+        x_banks = {}
+        made = {}
+        sums = {}
 
-        def load_inputs(u):
+        def load_norm_grad_x(u):
             norm_t = loads.tile([P, PACK, N_TILE], F32)
             grad_t = loads.tile([P, PACK, N_TILE], BF16)
             x_t = loads.tile([P, PACK, N_TILE], BF16)
@@ -76,66 +82,104 @@ def tile_gdn_t_v_kernel(tc, x, gamma, beta, norm, y, grad_out, out):
                 nc.sync.dma_start(out=norm_t[:, h, :], in_=dram_unit(norm_units, u)[:, h, :])
                 nc.sync.dma_start(out=grad_t[:, h, :], in_=dram_unit(grad_units, u)[:, h, :])
                 nc.sync.dma_start(out=x_t[:, h, :], in_=dram_unit(x_units, u)[:, h, :])
-            inputs[u] = (norm_t, grad_t, x_t)
+            raw[u] = [norm_t, grad_t, x_t]
 
-        def quantise_gamma():
-            for g in range(PASSES):
-                gamma_rows = stage.tile([P, PACK, CHANNELS], BF16)
-                nc.sync.dma_start(out=gamma_rows[:], in_=gamma_passes[g])
-                gamma_grouped = stage.tile([P, CHANNELS, PACK], BF16, align_bytes=64)
-                for c0 in range(0, CHANNELS, N_TILE):
-                    regroup(nc, gamma_grouped[:, c0 : c0 + N_TILE, :], gamma_rows[:, :, c0 : c0 + N_TILE])
-                nc.vector.quantize_mx(
-                    out=gamma_codes[:, g, :].bitcast(E4M3_X4),
-                    scales=gamma_scales[:, g, :],
-                    in_=gamma_grouped[:].rearrange("p c t -> p (c t)"),
-                )
+        def load_y(u):
+            result = results.tile([P, PACK, N_TILE], F32)
+            nc.sync.dma_start(out=result[:], in_=dram_unit(y_units, u))
+            raw[u].append(result)
 
-        def make_dn(u):
-            norm_t, grad_t, x_t = inputs[u]
+        def inverse_roots(u):
+            norm_t = raw[u][0]
             inv_root = short.tile([P, PACK, N_TILE], F32)
-            inv_norm = saved.tile([P, PACK, N_TILE], F32)
+            inv_norm = short.tile([P, PACK, N_TILE], F32)
             for h in HALVES:
                 nc.scalar.activation(out=inv_root[:, h, :], in_=norm_t[:, h, :], func=ACT.Abs_reciprocal_sqrt)
             for h in HALVES:
                 nc.scalar.activation(out=inv_norm[:, h, :], in_=inv_root[:, h, :], func=ACT.Square)
-            grad_over_norm = saved.tile([P, PACK, N_TILE], F32)
-            x_over_root = short.tile([P, PACK, N_TILE], F32)
-            dn = short.tile([P, PACK, N_TILE], BF16)
+            roots[u] = [inv_root, inv_norm]
+
+        def root(u):
+            inv_norm = roots[u][1]
+            root_t = once.tile([P, PACK, N_TILE], F32)
             for h in HALVES:
-                nc.vector.tensor_tensor(out=grad_over_norm[:, h, :], in0=grad_t[:, h, :], in1=inv_norm[:, h, :], op=ALU.mult)
-            helper = nc.gpsimd if u > LAG else nc.vector
-            nc.vector.tensor_tensor(out=x_over_root[:, HALVES[0], :], in0=x_t[:, HALVES[0], :], in1=inv_root[:, HALVES[0], :], op=ALU.mult)
-            helper.tensor_tensor(out=x_over_root[:, HALVES[1], :], in0=x_t[:, HALVES[1], :], in1=inv_root[:, HALVES[1], :], op=ALU.mult)
+                nc.scalar.activation(out=root_t[:, h, :], in_=inv_norm[:, h, :], func=ACT.Abs_reciprocal_sqrt)
+            roots[u].append(root_t)
+
+        def x_to_psum(u):
+            x_t = raw[u][2]
+            x_banks[u] = []
             for h in HALVES:
+                bank = psum_x.tile([P, PACK // 2, N_TILE], BF16)
+                for j in range(PACK // 2):
+                    nc.tensor.matmul(out=bank[:, j, :], lhsT=identity[:], rhs=x_t[:, h.start + j, :], start=True, stop=True)
+                x_banks[u].append(bank)
+
+        def quantise_gamma(g, gamma_rows):
+            gamma_grouped = stage.tile([P, CHANNELS, PACK], BF16, align_bytes=64)
+            for c0 in range(0, CHANNELS, N_TILE):
+                nc.scalar.copy(
+                    out=gamma_grouped[:, c0 : c0 + N_TILE, :].rearrange("p (c i) t -> p c t i", i=4),
+                    in_=gamma_rows[:, :, c0 : c0 + N_TILE].rearrange("p t (c i) -> p c t i", i=4),
+                )
+            nc.vector.quantize_mx(
+                out=gamma_codes[:, g, :].bitcast(E4M3_X4),
+                scales=gamma_scales[:, g, :],
+                in_=gamma_grouped[:].rearrange("p c t -> p (c t)"),
+            )
+
+        def make_first_term(u):
+            grad_t = raw[u][1]
+            inv_root = roots[u][0]
+            first = kept.tile([P, PACK, N_TILE], F32)
+            for h in HALVES:
+                nc.vector.tensor_tensor(out=first[:, h, :], in0=grad_t[:, h, :], in1=inv_root[:, h, :], op=ALU.mult)
+            made[u] = [first]
+
+        def make_x_over_norm(u):
+            inv_norm = roots[u][1]
+            x_over_norm = once.tile([P, PACK, N_TILE], F32)
+            for n, h in enumerate(HALVES):
+                x_half = x_banks[u][n][:] if u in x_banks else raw[u][2][:, h, :]
                 nc.vector.scalar_tensor_tensor(
-                    out=dn[:, h, :], in0=grad_over_norm[:, h, :], scalar=-0.5, in1=x_over_root[:, h, :],
+                    out=flat(x_over_norm[:, h, :]), in0=flat(x_half), scalar=-0.5, in1=flat(inv_norm[:, h, :]),
                     op0=ALU.mult, op1=ALU.mult,
                 )
+            made[u].append(x_over_norm)
+
+        def make_dn(u):
+            first, x_over_norm = made[u]
             dn_grouped = short.tile([P, N_TILE, PACK], BF16, align_bytes=64)
-            regroup(nc, dn_grouped[:], dn[:])
+            nc.vector.tensor_tensor(
+                out=dn_grouped[:].rearrange("p (c i) t -> p c t i", i=4),
+                in0=first[:].rearrange("p t (c i) -> p c t i", i=4),
+                in1=x_over_norm[:].rearrange("p t (c i) -> p c t i", i=4),
+                op=ALU.mult,
+            )
+            made[u].append(dn_grouped)
+
+        def quantise_dn(u):
             dn_codes = coded.tile([P, N_TILE], U32, align_bytes=64)
             dn_scales = coded.tile([P, N_TILE], U8, align_bytes=64)
             nc.vector.quantize_mx(
                 out=dn_codes[:].bitcast(E5M2_X4),
                 scales=dn_scales[:],
-                in_=dn_grouped[:].rearrange("p w t -> p (w t)"),
+                in_=made[u][2][:].rearrange("p w t -> p (w t)"),
             )
-            held[u] = (inv_norm, grad_over_norm, dn_codes, dn_scales)
+            made[u].append((dn_codes, dn_scales))
 
-        def finish(u):
+        def make_factor(u):
+            result = raw[u][3]
+            nc.vector.tensor_tensor(out=flat(result[:]), in0=flat(result[:]), in1=flat(roots[u][2][:]), op=ALU.mult)
+
+        def multiply(u):
             block, g_out = divmod(u, PASSES)
-            inv_norm, grad_over_norm = held[u][0:2]
-            result = short.tile([P, PACK, N_TILE], F32)
-            nc.sync.dma_start(out=result[:], in_=dram_unit(y_units, u))
-            root = short.tile([P, PACK, N_TILE], F32)
-            for h in HALVES:
-                nc.scalar.activation(out=root[:, h, :], in_=inv_norm[:, h, :], func=ACT.Abs_reciprocal_sqrt)
+            sums[u] = []
             for t in range(PACK):
                 c0 = (g_out * PACK + t) * P
-                m = psum.tile([P, N_TILE], F32)
+                m = psum_m.tile([P, N_TILE], F32)
                 for g in range(PASSES):
-                    dn_codes, dn_scales = held[block * PASSES + g][2:4]
+                    dn_codes, dn_scales = made[block * PASSES + g][3]
                     nc.tensor.matmul_mx(
                         out=m[:],
                         lhsT=gamma_codes[:, g, c0 : c0 + P].bitcast(E4M3_X4),
@@ -145,22 +189,75 @@ def tile_gdn_t_v_kernel(tc, x, gamma, beta, norm, y, grad_out, out):
                         start=(g == 0),
                         stop=(g == PASSES - 1),
                     )
-                nc.vector.scalar_tensor_tensor(
-                    out=result[:, t, :], in0=m[:], scalar=2.0, in1=result[:, t, :], op0=ALU.mult, op1=ALU.mult,
-                )
-            for h in HALVES:
-                nc.vector.tensor_tensor(out=result[:, h, :], in0=result[:, h, :], in1=grad_over_norm[:, h, :], op=ALU.add)
-            for h in HALVES:
-                nc.vector.tensor_tensor(out=result[:, h, :], in0=result[:, h, :], in1=root[:, h, :], op=ALU.mult)
-                nc.sync.dma_start(out=dram_unit(out_units, u)[:, h, :], in_=result[:, h, :])
+                sums[u].append(m)
 
-        for u in range(AHEAD):
-            load_inputs(u)
-        quantise_gamma()
-        for i in range(UNITS + LAG):
-            if i + AHEAD < UNITS:
-                load_inputs(i + AHEAD)
-            if i < UNITS:
+        def second_term(u):
+            result = raw[u][3]
+            for t in range(PACK):
+                nc.vector.scalar_tensor_tensor(
+                    out=result[:, t, :], in0=sums[u][t][:], scalar=2.0, in1=result[:, t, :], op0=ALU.mult, op1=ALU.mult,
+                )
+
+        def add_terms(engine, u, t):
+            result = raw[u][3]
+            engine.tensor_tensor(out=result[:, t, :], in0=result[:, t, :], in1=made[u][0][:, t, :], op=ALU.add)
+
+        def store(u, t):
+            nc.sync.dma_start(out=dram_unit(out_units, u)[:, t, :], in_=raw[u][3][:, t, :])
+
+        with tc.manual_schedule():
+            for u in range(AHEAD):
+                load_norm_grad_x(u)
+            gamma_loaded = []
+            for g in range(PASSES):
+                gamma_rows = stage.tile([P, PACK, CHANNELS], BF16)
+                nc.sync.dma_start(out=gamma_rows[:], in_=gamma_passes[g])
+                gamma_loaded.append(gamma_rows)
+            for u in range(AHEAD):
+                load_y(u)
+                inverse_roots(u)
+
+            for i in range(UNITS):
+                if i + AHEAD < UNITS:
+                    load_norm_grad_x(i + AHEAD)
+                    load_y(i + AHEAD)
+                if i >= LAG:
+                    multiply(i - LAG)
+                if LAG <= i + 1 < UNITS:
+                    x_to_psum(i + 1)
+                if i >= LAG:
+                    root(i)
+                    if i + 1 < UNITS:
+                        inverse_roots(i + 1)
+                make_first_term(i)
+                if i >= LAG:
+                    second_term(i - LAG)
+                make_x_over_norm(i)
+                if i >= LAG:
+                    for t in range(PACK - 1):
+                        add_terms(nc.gpsimd, i - LAG, t)
                 make_dn(i)
-            if i >= LAG:
-                finish(i - LAG)
+                if i >= LAG:
+                    make_factor(i)
+                    add_terms(nc.vector, i - LAG, PACK - 1)
+                    for h in HALVES:
+                        store(i - LAG, h)
+                quantise_dn(i)
+                if i == LAG - 1:
+                    for u in range(LAG):
+                        quantise_gamma(u, gamma_loaded[u])
+                        root(u)
+                        make_factor(u)
+                    inverse_roots(LAG)
+
+            for u in (UNITS - 2, UNITS - 1):
+                multiply(u)
+                second_term(u)
+            for t in range(PACK - 1):
+                add_terms(nc.gpsimd, UNITS - 2, t)
+            add_terms(nc.vector, UNITS - 2, PACK - 1)
+            for h in HALVES:
+                store(UNITS - 2, h)
+            for t in range(PACK):
+                add_terms(nc.vector, UNITS - 1, t)
+                store(UNITS - 1, slice(t, t + 1))

@@ -22,7 +22,7 @@ PASSES = CHANNELS // K_PASS
 N_TILE = 512
 BLOCKS = BATCH * PIXELS // N_TILE
 UNITS = BLOCKS * PASSES
-LAG = 2
+LAG = 3
 AHEAD = 2
 HALVES = (slice(0, PACK // 2), slice(PACK // 2, PACK))
 
@@ -54,23 +54,27 @@ def tile_gdn_t_v_kernel(tc, x, gamma, beta, norm, y, grad_out, out):
     with ExitStack() as stack:
         keep = stack.enter_context(tc.tile_pool(name="keep", bufs=1))
         stage = stack.enter_context(tc.tile_pool(name="stage", bufs=PASSES))
-        loads = stack.enter_context(tc.tile_pool(name="loads", bufs=3))
+        loads = stack.enter_context(tc.tile_pool(name="loads", bufs=AHEAD))
         short = stack.enter_context(tc.tile_pool(name="short", bufs=2))
         once = stack.enter_context(tc.tile_pool(name="once", bufs=1))
         kept = stack.enter_context(tc.tile_pool(name="kept", bufs=LAG + 2))
-        results = stack.enter_context(tc.tile_pool(name="results", bufs=LAG + 3))
+        results = stack.enter_context(tc.tile_pool(name="results", bufs=LAG + 2))
         coded = stack.enter_context(tc.tile_pool(name="coded", bufs=LAG + 3))
-        psum_m = stack.enter_context(tc.psum_pool(name="psum_m", bufs=4))
-        psum_x = stack.enter_context(tc.psum_pool(name="psum_x", bufs=4))
+        psum_m = stack.enter_context(tc.psum_pool(name="psum_m", bufs=PACK))
+        psum_x = stack.enter_context(tc.psum_pool(name="psum_x", bufs=len(HALVES)))
+        psum_g = stack.enter_context(tc.psum_pool(name="psum_g", bufs=len(HALVES)))
 
         gamma_codes = keep.tile([P, PASSES, CHANNELS], U32, align_bytes=64)
         gamma_scales = keep.tile([P, PASSES, CHANNELS], U8, align_bytes=64)
         identity = keep.tile([P, P], BF16)
         make_identity(nc, identity[:])
+        identity_words = keep.tile([P, P], F32)
+        make_identity(nc, identity_words[:])
 
         raw = {}
         roots = {}
         x_banks = {}
+        grad_banks = {}
         made = {}
         sums = {}
 
@@ -89,39 +93,77 @@ def tile_gdn_t_v_kernel(tc, x, gamma, beta, norm, y, grad_out, out):
             nc.sync.dma_start(out=result[:], in_=dram_unit(y_units, u))
             raw[u].append(result)
 
-        def inverse_roots(u):
+        def inverse_root(u):
             norm_t = raw[u][0]
             inv_root = short.tile([P, PACK, N_TILE], F32)
-            inv_norm = short.tile([P, PACK, N_TILE], F32)
             for h in HALVES:
                 nc.scalar.activation(out=inv_root[:, h, :], in_=norm_t[:, h, :], func=ACT.Abs_reciprocal_sqrt)
+            roots[u] = [inv_root]
+
+        def inverse_norm(u):
+            inv_norm = short.tile([P, PACK, N_TILE], F32)
             for h in HALVES:
-                nc.scalar.activation(out=inv_norm[:, h, :], in_=inv_root[:, h, :], func=ACT.Square)
-            roots[u] = [inv_root, inv_norm]
+                nc.scalar.activation(out=inv_norm[:, h, :], in_=roots[u][0][:, h, :], func=ACT.Square)
+            roots[u].append(inv_norm)
 
         def root(u):
             inv_norm = roots[u][1]
-            root_t = once.tile([P, PACK, N_TILE], F32)
+            root_t = short.tile([P, PACK, N_TILE], F32)
             for h in HALVES:
                 nc.scalar.activation(out=root_t[:, h, :], in_=inv_norm[:, h, :], func=ACT.Abs_reciprocal_sqrt)
             roots[u].append(root_t)
+
+        def grad_words(u):
+            return flat(raw[u][1][:]).bitcast(F32)
+
+        def turn_grad(u, n):
+            words = grad_words(u)
+            turned_bank = psum_x.tile([P, PACK, P], F32, tag="bank")
+            for k in range(PACK):
+                w0 = (n * PACK + k) * P
+                nc.tensor.transpose(turned_bank[:, k, :], words[:, w0 : w0 + P], identity_words[:])
+            return turned_bank
+
+        def copy_turned(turned_bank):
+            turned = short.tile([P, PACK, P], F32)
+            nc.scalar.copy(out=turned[:], in_=turned_bank[:])
+            return turned
+
+        def turn_back(u, turned):
+            bank = psum_g.tile([P, PACK, P], F32, tag="bank")
+            for k in range(PACK):
+                nc.tensor.transpose(bank[:, k, :], turned[:, k, :], identity_words[:])
+            grad_banks.setdefault(u, []).append(bank)
+
+        def stage_grad(u):
+            banks = [turn_grad(u, n) for n in range(len(HALVES))]
+            for bank in banks:
+                turn_back(u, copy_turned(bank))
 
         def x_to_psum(u):
             x_t = raw[u][2]
             x_banks[u] = []
             for h in HALVES:
-                bank = psum_x.tile([P, PACK // 2, N_TILE], BF16)
+                bank = psum_x.tile([P, PACK // 2, N_TILE], BF16, tag="bank")
                 for j in range(PACK // 2):
                     nc.tensor.matmul(out=bank[:, j, :], lhsT=identity[:], rhs=x_t[:, h.start + j, :], start=True, stop=True)
                 x_banks[u].append(bank)
 
-        def quantise_gamma(g, gamma_rows):
-            gamma_grouped = stage.tile([P, CHANNELS, PACK], BF16, align_bytes=64)
+        def load_gamma(g):
+            gamma_rows = stage.tile([P, PACK, CHANNELS], BF16)
+            nc.sync.dma_start(out=gamma_rows[:], in_=gamma_passes[g])
+            return gamma_rows
+
+        def regroup_gamma(gamma_rows):
+            gamma_grouped = once.tile([P, CHANNELS, PACK], BF16, align_bytes=64)
             for c0 in range(0, CHANNELS, N_TILE):
                 nc.scalar.copy(
                     out=gamma_grouped[:, c0 : c0 + N_TILE, :].rearrange("p (c i) t -> p c t i", i=4),
                     in_=gamma_rows[:, :, c0 : c0 + N_TILE].rearrange("p t (c i) -> p c t i", i=4),
                 )
+            return gamma_grouped
+
+        def quantise_gamma(g, gamma_grouped):
             nc.vector.quantize_mx(
                 out=gamma_codes[:, g, :].bitcast(E4M3_X4),
                 scales=gamma_scales[:, g, :],
@@ -132,8 +174,12 @@ def tile_gdn_t_v_kernel(tc, x, gamma, beta, norm, y, grad_out, out):
             grad_t = raw[u][1]
             inv_root = roots[u][0]
             first = kept.tile([P, PACK, N_TILE], F32)
-            for h in HALVES:
-                nc.vector.tensor_tensor(out=first[:, h, :], in0=grad_t[:, h, :], in1=inv_root[:, h, :], op=ALU.mult)
+            for n, h in enumerate(HALVES):
+                if u in grad_banks:
+                    grad_half = grad_banks[u][n][:].rearrange("p k w -> p (k w)").bitcast(BF16)
+                else:
+                    grad_half = flat(grad_t[:, h, :])
+                nc.vector.tensor_tensor(out=flat(first[:, h, :]), in0=grad_half, in1=flat(inv_root[:, h, :]), op=ALU.mult)
             made[u] = [first]
 
         def make_x_over_norm(u):
@@ -168,16 +214,16 @@ def tile_gdn_t_v_kernel(tc, x, gamma, beta, norm, y, grad_out, out):
             )
             made[u].append((dn_codes, dn_scales))
 
-        def make_factor(u):
-            result = raw[u][3]
-            nc.vector.tensor_tensor(out=flat(result[:]), in0=flat(result[:]), in1=flat(roots[u][2][:]), op=ALU.mult)
+        def make_factor(engine, u, first_column, end_column):
+            w = slice(first_column, end_column)
+            result = flat(raw[u][3][:])
+            engine.tensor_tensor(out=result[:, w], in0=result[:, w], in1=flat(roots[u][2][:])[:, w], op=ALU.mult)
 
-        def multiply(u):
+        def multiply(u, slots, pools):
             block, g_out = divmod(u, PASSES)
-            sums[u] = []
-            for t in range(PACK):
+            for t in slots:
                 c0 = (g_out * PACK + t) * P
-                m = psum_m.tile([P, N_TILE], F32)
+                m = pools[t].tile([P, N_TILE], F32, tag="bank")
                 for g in range(PASSES):
                     dn_codes, dn_scales = made[block * PASSES + g][3]
                     nc.tensor.matmul_mx(
@@ -189,75 +235,118 @@ def tile_gdn_t_v_kernel(tc, x, gamma, beta, norm, y, grad_out, out):
                         start=(g == 0),
                         stop=(g == PASSES - 1),
                     )
-                sums[u].append(m)
+                sums.setdefault(u, []).append(m)
 
-        def second_term(u):
+        def second_term(u, slots):
             result = raw[u][3]
-            for t in range(PACK):
+            for t in slots:
                 nc.vector.scalar_tensor_tensor(
                     out=result[:, t, :], in0=sums[u][t][:], scalar=2.0, in1=result[:, t, :], op0=ALU.mult, op1=ALU.mult,
                 )
 
-        def add_terms(engine, u, t):
+        def add_terms(engine, u, s):
             result = raw[u][3]
-            engine.tensor_tensor(out=result[:, t, :], in0=result[:, t, :], in1=made[u][0][:, t, :], op=ALU.add)
+            engine.tensor_tensor(out=flat(result[:, s, :]), in0=flat(result[:, s, :]), in1=flat(made[u][0][:, s, :]), op=ALU.add)
 
-        def store(u, t):
-            nc.sync.dma_start(out=dram_unit(out_units, u)[:, t, :], in_=raw[u][3][:, t, :])
+        def store(u, s):
+            nc.sync.dma_start(out=dram_unit(out_units, u)[:, s, :], in_=raw[u][3][:, s, :])
 
         with tc.manual_schedule():
-            for u in range(AHEAD):
-                load_norm_grad_x(u)
-            gamma_loaded = []
-            for g in range(PASSES):
-                gamma_rows = stage.tile([P, PACK, CHANNELS], BF16)
-                nc.sync.dma_start(out=gamma_rows[:], in_=gamma_passes[g])
-                gamma_loaded.append(gamma_rows)
-            for u in range(AHEAD):
-                load_y(u)
-                inverse_roots(u)
+            slot = [slice(t, t + 1) for t in range(PACK)]
+            thirds = (slot[0], slice(1, PACK - 1), slot[PACK - 1])
+            usual = [psum_m] * PACK
+            cut = (N_TILE // 2, 2 * N_TILE, PACK * N_TILE)
+            load_norm_grad_x(0)
+            load_norm_grad_x(1)
+            inverse_root(0)
+            inverse_norm(0)
+            make_first_term(0)
+            make_x_over_norm(0)
+            make_dn(0)
+            load_norm_grad_x(2)
+            load_y(0)
+            gamma_rows_0 = load_gamma(0)
+            gamma_rows_1 = load_gamma(1)
+            inverse_root(1)
+            inverse_norm(1)
+            make_first_term(1)
+            quantise_dn(0)
+            make_x_over_norm(1)
+            make_dn(1)
+            load_norm_grad_x(3)
+            load_y(1)
+            load_y(2)
+            inverse_root(2)
+            stage_grad(2)
+            x_to_psum(2)
+            root(0)
+            inverse_norm(2)
+            gamma_grouped_0 = regroup_gamma(gamma_rows_0)
+            make_first_term(2)
+            quantise_dn(1)
+            make_x_over_norm(2)
+            make_factor(nc.gpsimd, 0, 0, 3 * N_TILE)
+            quantise_gamma(0, gamma_grouped_0)
+            gamma_grouped_1 = regroup_gamma(gamma_rows_1)
+            make_dn(2)
+            make_factor(nc.vector, 0, 3 * N_TILE, 4 * N_TILE)
+            quantise_dn(2)
+            quantise_gamma(1, gamma_grouped_1)
+            root(1)
+            make_factor(nc.vector, 1, 0, 4 * N_TILE)
+            load_norm_grad_x(4)
+            load_y(3)
+            root(2)
+            make_factor(nc.vector, 2, 0, 4 * N_TILE)
+            multiply(0, range(PACK), usual)
+            inverse_root(3)
+            stage_grad(3)
+            inverse_norm(3)
+            x_to_psum(3)
 
-            for i in range(UNITS):
-                if i + AHEAD < UNITS:
-                    load_norm_grad_x(i + AHEAD)
-                    load_y(i + AHEAD)
-                if i >= LAG:
-                    multiply(i - LAG)
-                if LAG <= i + 1 < UNITS:
-                    x_to_psum(i + 1)
-                if i >= LAG:
-                    root(i)
-                    if i + 1 < UNITS:
-                        inverse_roots(i + 1)
+            for i in range(LAG, UNITS):
+                u = i - LAG
+                if i + 2 < UNITS:
+                    load_norm_grad_x(i + 2)
+                if i + 1 < UNITS:
+                    load_y(i + 1)
+                root(i)
+                second_term(u, range(PACK))
                 make_first_term(i)
-                if i >= LAG:
-                    second_term(i - LAG)
                 make_x_over_norm(i)
-                if i >= LAG:
-                    for t in range(PACK - 1):
-                        add_terms(nc.gpsimd, i - LAG, t)
+                multiply(u + 1, range(PACK), usual)
+                if i + 1 < UNITS:
+                    inverse_root(i + 1)
+                    stage_grad(i + 1)
+                    inverse_norm(i + 1)
+                    x_to_psum(i + 1)
+                for s in thirds:
+                    add_terms(nc.gpsimd, u, s)
+                make_factor(nc.gpsimd, i, 0, cut[0])
                 make_dn(i)
-                if i >= LAG:
-                    make_factor(i)
-                    add_terms(nc.vector, i - LAG, PACK - 1)
-                    for h in HALVES:
-                        store(i - LAG, h)
+                make_factor(nc.vector, i, cut[0], cut[1])
                 quantise_dn(i)
-                if i == LAG - 1:
-                    for u in range(LAG):
-                        quantise_gamma(u, gamma_loaded[u])
-                        root(u)
-                        make_factor(u)
-                    inverse_roots(LAG)
+                make_factor(nc.vector, i, cut[1], cut[2])
+                for h in HALVES:
+                    store(u, h)
 
-            for u in (UNITS - 2, UNITS - 1):
-                multiply(u)
-                second_term(u)
-            for t in range(PACK - 1):
-                add_terms(nc.gpsimd, UNITS - 2, t)
-            add_terms(nc.vector, UNITS - 2, PACK - 1)
+            a, b, c = UNITS - 3, UNITS - 2, UNITS - 1
+            second_term(a, range(PACK))
+            multiply(b, range(PACK), [psum_x, psum_x, psum_g, psum_g])
+            multiply(c, range(PACK), usual)
+            second_term(b, range(PACK))
+            second_term(c, range(PACK))
+            for s in thirds:
+                add_terms(nc.gpsimd, a, s)
+            add_terms(nc.gpsimd, b, slot[0])
             for h in HALVES:
-                store(UNITS - 2, h)
-            for t in range(PACK):
-                add_terms(nc.vector, UNITS - 1, t)
-                store(UNITS - 1, slice(t, t + 1))
+                store(a, h)
+            add_terms(nc.vector, c, slot[PACK - 1])
+            add_terms(nc.vector, b, slot[1])
+            store(c, slot[PACK - 1])
+            store(b, HALVES[0])
+            add_terms(nc.vector, b, HALVES[1])
+            store(b, HALVES[1])
+            for t in range(PACK - 1):
+                add_terms(nc.vector, c, slot[t])
+                store(c, slot[t])

@@ -273,9 +273,9 @@ def tile_gdn_t_v_kernel(tc, x, gamma, beta, norm, y, grad_out, out):
             quantise_dn(0)
             make_x_over_norm(1)
             make_dn(1)
-            load_norm_grad_x(3)
             load_y(1)
             load_y(2)
+            load_norm_grad_x(3)
             inverse_root(2)
             stage_grad(2)
             x_to_psum(2)

@@ -113,14 +113,10 @@ def tile_gdn_t_v_kernel(tc, x, gamma, beta, norm, y, grad_out, out):
                 nc.scalar.activation(out=root_t[:, h, :], in_=inv_norm[:, h, :], func=ACT.Abs_reciprocal_sqrt)
             roots[u].append(root_t)
 
-        def grad_words(u):
-            return flat(raw[u][1][:]).bitcast(F32)
-
-        def turn_grad(u, n):
-            words = grad_words(u)
-            turned_bank = psum_x.tile([P, PACK, P], F32, tag="bank")
+        def turn(pool, words, first_word):
+            turned_bank = pool.tile([P, PACK, P], F32, tag="bank")
             for k in range(PACK):
-                w0 = (n * PACK + k) * P
+                w0 = first_word + k * P
                 nc.tensor.transpose(turned_bank[:, k, :], words[:, w0 : w0 + P], identity_words[:])
             return turned_bank
 
@@ -129,16 +125,16 @@ def tile_gdn_t_v_kernel(tc, x, gamma, beta, norm, y, grad_out, out):
             nc.scalar.copy(out=turned[:], in_=turned_bank[:])
             return turned
 
-        def turn_back(u, turned):
+        def turn_back(turned):
             bank = psum_g.tile([P, PACK, P], F32, tag="bank")
             for k in range(PACK):
                 nc.tensor.transpose(bank[:, k, :], turned[:, k, :], identity_words[:])
-            grad_banks.setdefault(u, []).append(bank)
+            return bank
 
         def stage_grad(u):
-            banks = [turn_grad(u, n) for n in range(len(HALVES))]
-            for bank in banks:
-                turn_back(u, copy_turned(bank))
+            words = flat(raw[u][1][:]).bitcast(F32)
+            banks = [turn(psum_x, words, n * N_TILE) for n in range(len(HALVES))]
+            grad_banks[u] = [turn_back(copy_turned(bank)) for bank in banks]
 
         def x_to_psum(u):
             x_t = raw[u][2]
@@ -219,6 +215,11 @@ def tile_gdn_t_v_kernel(tc, x, gamma, beta, norm, y, grad_out, out):
             result = flat(raw[u][3][:])
             engine.tensor_tensor(out=result[:, w], in0=result[:, w], in1=flat(roots[u][2][:])[:, w], op=ALU.mult)
 
+        def make_factor_from_psum(u, t, bank):
+            nc.vector.tensor_tensor(
+                out=raw[u][3][:, t, :], in0=bank[:].rearrange("p k w -> p (k w)"), in1=roots[u][2][:, t, :], op=ALU.mult,
+            )
+
         def multiply(u, slots, pools):
             block, g_out = divmod(u, PASSES)
             for t in slots:
@@ -255,7 +256,6 @@ def tile_gdn_t_v_kernel(tc, x, gamma, beta, norm, y, grad_out, out):
             slot = [slice(t, t + 1) for t in range(PACK)]
             thirds = (slot[0], slice(1, PACK - 1), slot[PACK - 1])
             usual = [psum_m] * PACK
-            cut = (N_TILE // 2, 2 * N_TILE, PACK * N_TILE)
             load_norm_grad_x(0)
             load_norm_grad_x(1)
             inverse_root(0)
@@ -312,9 +312,15 @@ def tile_gdn_t_v_kernel(tc, x, gamma, beta, norm, y, grad_out, out):
                     load_y(i + 1)
                 root(i)
                 second_term(u, range(PACK))
+                y_words = flat(raw[i][3][:])
+                turned = [turn(psum_m, y_words, t * N_TILE) for t in (2, 3)]
+                multiply(u + 1, range(2), usual)
                 make_first_term(i)
+                y_banks = [turn_back(copy_turned(bank)) for bank in turned]
+                multiply(u + 1, range(2, PACK), usual)
                 make_x_over_norm(i)
-                multiply(u + 1, range(PACK), usual)
+                for n in range(2):
+                    make_factor_from_psum(i, 2 + n, y_banks[n])
                 if i + 1 < UNITS:
                     inverse_root(i + 1)
                     stage_grad(i + 1)
@@ -322,11 +328,10 @@ def tile_gdn_t_v_kernel(tc, x, gamma, beta, norm, y, grad_out, out):
                     x_to_psum(i + 1)
                 for s in thirds:
                     add_terms(nc.gpsimd, u, s)
-                make_factor(nc.gpsimd, i, 0, cut[0])
+                make_factor(nc.gpsimd, i, 0, 3 * N_TILE // 2)
                 make_dn(i)
-                make_factor(nc.vector, i, cut[0], cut[1])
+                make_factor(nc.vector, i, 3 * N_TILE // 2, 2 * N_TILE)
                 quantise_dn(i)
-                make_factor(nc.vector, i, cut[1], cut[2])
                 for h in HALVES:
                     store(u, h)
 

@@ -25,6 +25,7 @@ UNITS = BLOCKS * PASSES
 LAG = 3
 AHEAD = 2
 HALVES = (slice(0, PACK // 2), slice(PACK // 2, PACK))
+QUARTERS = tuple(slice(t, t + 1) for t in range(PACK))
 
 FLOPS = 2 * BATCH * PIXELS * CHANNELS * CHANNELS
 
@@ -54,6 +55,7 @@ def tile_gdn_t_v_kernel(tc, x, gamma, beta, norm, y, grad_out, out):
     with ExitStack() as stack:
         keep = stack.enter_context(tc.tile_pool(name="keep", bufs=1))
         stage = stack.enter_context(tc.tile_pool(name="stage", bufs=PASSES))
+        grouping = stack.enter_context(tc.tile_pool(name="grouping", bufs=3))
         loads = stack.enter_context(tc.tile_pool(name="loads", bufs=AHEAD))
         short = stack.enter_context(tc.tile_pool(name="short", bufs=2))
         once = stack.enter_context(tc.tile_pool(name="once", bufs=1))
@@ -78,13 +80,17 @@ def tile_gdn_t_v_kernel(tc, x, gamma, beta, norm, y, grad_out, out):
         made = {}
         sums = {}
 
+        def pieces(u, h):
+            return QUARTERS[h] if u == 0 and h == HALVES[0] else (h,)
+
         def load_norm_grad_x(u):
             norm_t = loads.tile([P, PACK, N_TILE], F32)
             grad_t = loads.tile([P, PACK, N_TILE], BF16)
             x_t = loads.tile([P, PACK, N_TILE], BF16)
             for h in HALVES:
-                nc.sync.dma_start(out=norm_t[:, h, :], in_=dram_unit(norm_units, u)[:, h, :])
-                nc.sync.dma_start(out=grad_t[:, h, :], in_=dram_unit(grad_units, u)[:, h, :])
+                for s in pieces(u, h):
+                    nc.sync.dma_start(out=norm_t[:, s, :], in_=dram_unit(norm_units, u)[:, s, :])
+                    nc.sync.dma_start(out=grad_t[:, s, :], in_=dram_unit(grad_units, u)[:, s, :])
                 nc.sync.dma_start(out=x_t[:, h, :], in_=dram_unit(x_units, u)[:, h, :])
             raw[u] = [norm_t, grad_t, x_t]
 
@@ -93,18 +99,19 @@ def tile_gdn_t_v_kernel(tc, x, gamma, beta, norm, y, grad_out, out):
             nc.sync.dma_start(out=result[:], in_=dram_unit(y_units, u))
             raw[u].append(result)
 
-        def inverse_root(u):
-            norm_t = raw[u][0]
+        def new_roots(u):
             inv_root = short.tile([P, PACK, N_TILE], F32)
-            for h in HALVES:
-                nc.scalar.activation(out=inv_root[:, h, :], in_=norm_t[:, h, :], func=ACT.Abs_reciprocal_sqrt)
-            roots[u] = [inv_root]
-
-        def inverse_norm(u):
             inv_norm = short.tile([P, PACK, N_TILE], F32)
-            for h in HALVES:
-                nc.scalar.activation(out=inv_norm[:, h, :], in_=roots[u][0][:, h, :], func=ACT.Square)
-            roots[u].append(inv_norm)
+            roots[u] = [inv_root, inv_norm]
+
+        def inverse_root(u, halves=HALVES):
+            for h in halves:
+                for s in pieces(u, h):
+                    nc.scalar.activation(out=roots[u][0][:, s, :], in_=raw[u][0][:, s, :], func=ACT.Abs_reciprocal_sqrt)
+
+        def inverse_norm(u, halves=HALVES):
+            for h in halves:
+                nc.scalar.activation(out=roots[u][1][:, h, :], in_=roots[u][0][:, h, :], func=ACT.Square)
 
         def root(u):
             inv_norm = roots[u][1]
@@ -150,44 +157,47 @@ def tile_gdn_t_v_kernel(tc, x, gamma, beta, norm, y, grad_out, out):
             nc.sync.dma_start(out=gamma_rows[:], in_=gamma_passes[g])
             return gamma_rows
 
-        def regroup_gamma(gamma_rows):
-            gamma_grouped = once.tile([P, CHANNELS, PACK], BF16, align_bytes=64)
-            for c0 in range(0, CHANNELS, N_TILE):
-                nc.scalar.copy(
-                    out=gamma_grouped[:, c0 : c0 + N_TILE, :].rearrange("p (c i) t -> p c t i", i=4),
-                    in_=gamma_rows[:, :, c0 : c0 + N_TILE].rearrange("p t (c i) -> p c t i", i=4),
-                )
+        def regroup_gamma(gamma_rows, part):
+            c = slice(part * N_TILE, (part + 1) * N_TILE)
+            gamma_grouped = grouping.tile([P, N_TILE, PACK], BF16, align_bytes=64)
+            nc.scalar.copy(
+                out=gamma_grouped[:].rearrange("p (c i) t -> p c t i", i=4),
+                in_=gamma_rows[:, :, c].rearrange("p t (c i) -> p c t i", i=4),
+            )
             return gamma_grouped
 
-        def quantise_gamma(g, gamma_grouped):
+        def quantise_gamma(g, part, gamma_grouped):
+            c = slice(part * N_TILE, (part + 1) * N_TILE)
             nc.vector.quantize_mx(
-                out=gamma_codes[:, g, :].bitcast(E4M3_X4),
-                scales=gamma_scales[:, g, :],
+                out=gamma_codes[:, g, c].bitcast(E4M3_X4),
+                scales=gamma_scales[:, g, c],
                 in_=gamma_grouped[:].rearrange("p c t -> p (c t)"),
             )
 
-        def make_first_term(u):
-            grad_t = raw[u][1]
-            inv_root = roots[u][0]
+        def new_unit(u):
             first = kept.tile([P, PACK, N_TILE], F32)
-            for n, h in enumerate(HALVES):
-                if u in grad_banks:
-                    grad_half = grad_banks[u][n][:].rearrange("p k w -> p (k w)").bitcast(BF16)
-                else:
-                    grad_half = flat(grad_t[:, h, :])
-                nc.vector.tensor_tensor(out=flat(first[:, h, :]), in0=grad_half, in1=flat(inv_root[:, h, :]), op=ALU.mult)
-            made[u] = [first]
-
-        def make_x_over_norm(u):
-            inv_norm = roots[u][1]
             x_over_norm = once.tile([P, PACK, N_TILE], F32)
-            for n, h in enumerate(HALVES):
+            made[u] = [first, x_over_norm]
+
+        def make_first_term(u, halves=(0, 1)):
+            for n in halves:
+                for s in pieces(u, HALVES[n]):
+                    if u in grad_banks:
+                        grad_part = grad_banks[u][n][:].rearrange("p k w -> p (k w)").bitcast(BF16)
+                    else:
+                        grad_part = flat(raw[u][1][:, s, :])
+                    nc.vector.tensor_tensor(
+                        out=flat(made[u][0][:, s, :]), in0=grad_part, in1=flat(roots[u][0][:, s, :]), op=ALU.mult,
+                    )
+
+        def make_x_over_norm(u, halves=(0, 1)):
+            for n in halves:
+                h = HALVES[n]
                 x_half = x_banks[u][n][:] if u in x_banks else raw[u][2][:, h, :]
                 nc.vector.scalar_tensor_tensor(
-                    out=flat(x_over_norm[:, h, :]), in0=flat(x_half), scalar=-0.5, in1=flat(inv_norm[:, h, :]),
+                    out=flat(made[u][1][:, h, :]), in0=flat(x_half), scalar=-0.5, in1=flat(roots[u][1][:, h, :]),
                     op0=ALU.mult, op1=ALU.mult,
                 )
-            made[u].append(x_over_norm)
 
         def make_dn(u):
             first, x_over_norm = made[u]
@@ -258,15 +268,20 @@ def tile_gdn_t_v_kernel(tc, x, gamma, beta, norm, y, grad_out, out):
             usual = [psum_m] * PACK
             load_norm_grad_x(0)
             load_norm_grad_x(1)
-            inverse_root(0)
-            inverse_norm(0)
-            make_first_term(0)
-            make_x_over_norm(0)
+            new_roots(0)
+            new_unit(0)
+            for n in range(len(HALVES)):
+                inverse_root(0, HALVES[n : n + 1])
+                inverse_norm(0, HALVES[n : n + 1])
+                make_first_term(0, (n,))
+                make_x_over_norm(0, (n,))
             make_dn(0)
             load_norm_grad_x(2)
             load_y(0)
             gamma_rows_0 = load_gamma(0)
             gamma_rows_1 = load_gamma(1)
+            new_roots(1)
+            new_unit(1)
             inverse_root(1)
             inverse_norm(1)
             make_first_term(1)
@@ -274,31 +289,36 @@ def tile_gdn_t_v_kernel(tc, x, gamma, beta, norm, y, grad_out, out):
             make_x_over_norm(1)
             make_dn(1)
             load_y(1)
-            load_y(2)
             load_norm_grad_x(3)
+            load_y(2)
+            new_roots(2)
+            new_unit(2)
             inverse_root(2)
             stage_grad(2)
             x_to_psum(2)
             root(0)
             inverse_norm(2)
-            gamma_grouped_0 = regroup_gamma(gamma_rows_0)
             make_first_term(2)
-            quantise_dn(1)
             make_x_over_norm(2)
             make_factor(nc.gpsimd, 0, 0, 3 * N_TILE)
-            quantise_gamma(0, gamma_grouped_0)
-            gamma_grouped_1 = regroup_gamma(gamma_rows_1)
+            quantise_dn(1)
+            grouped = regroup_gamma(gamma_rows_0, 0)
+            quantise_gamma(0, 0, grouped)
             make_dn(2)
-            make_factor(nc.vector, 0, 3 * N_TILE, 4 * N_TILE)
+            grouped = regroup_gamma(gamma_rows_0, 1)
+            quantise_gamma(0, 1, grouped)
+            grouped = regroup_gamma(gamma_rows_1, 0)
             quantise_dn(2)
-            quantise_gamma(1, gamma_grouped_1)
+            quantise_gamma(1, 0, grouped)
             root(1)
             make_factor(nc.vector, 1, 0, 4 * N_TILE)
+            grouped = regroup_gamma(gamma_rows_1, 1)
+            quantise_gamma(1, 1, grouped)
+            make_factor(nc.vector, 0, 3 * N_TILE, 4 * N_TILE)
             load_norm_grad_x(4)
             load_y(3)
-            root(2)
-            make_factor(nc.vector, 2, 0, 4 * N_TILE)
             multiply(0, range(PACK), usual)
+            new_roots(3)
             inverse_root(3)
             stage_grad(3)
             inverse_norm(3)
@@ -310,18 +330,25 @@ def tile_gdn_t_v_kernel(tc, x, gamma, beta, norm, y, grad_out, out):
                     load_norm_grad_x(i + 2)
                 if i + 1 < UNITS:
                     load_y(i + 1)
-                root(i)
+                new_unit(i)
+                if i > LAG:
+                    root(i)
                 second_term(u, range(PACK))
                 y_words = flat(raw[i][3][:])
                 turned = [turn(psum_m, y_words, t * N_TILE) for t in (2, 3)]
                 multiply(u + 1, range(2), usual)
                 make_first_term(i)
                 y_banks = [turn_back(copy_turned(bank)) for bank in turned]
+                if i == LAG:
+                    root(i)
                 multiply(u + 1, range(2, PACK), usual)
                 make_x_over_norm(i)
                 for n in range(2):
                     make_factor_from_psum(i, 2 + n, y_banks[n])
+                if i == LAG:
+                    root(i - 1)
                 if i + 1 < UNITS:
+                    new_roots(i + 1)
                     inverse_root(i + 1)
                     stage_grad(i + 1)
                     inverse_norm(i + 1)
@@ -332,6 +359,8 @@ def tile_gdn_t_v_kernel(tc, x, gamma, beta, norm, y, grad_out, out):
                 make_dn(i)
                 make_factor(nc.vector, i, 3 * N_TILE // 2, 2 * N_TILE)
                 quantise_dn(i)
+                if i == LAG:
+                    make_factor(nc.vector, i - 1, 0, 4 * N_TILE)
                 for h in HALVES:
                     store(u, h)
 

@@ -94,10 +94,12 @@ def tile_gdn_t_v_kernel(tc, x, gamma, beta, norm, y, grad_out, out):
                 nc.sync.dma_start(out=x_t[:, h, :], in_=dram_unit(x_units, u)[:, h, :])
             raw[u] = [norm_t, grad_t, x_t]
 
-        def load_y(u):
+        def new_result(u):
             result = results.tile([P, PACK, N_TILE], F32)
-            nc.sync.dma_start(out=result[:], in_=dram_unit(y_units, u))
             raw[u].append(result)
+
+        def load_y(u):
+            nc.sync.dma_start(out=raw[u][3][:], in_=dram_unit(y_units, u))
 
         def new_roots(u):
             inv_root = short.tile([P, PACK, N_TILE], F32)
@@ -277,6 +279,7 @@ def tile_gdn_t_v_kernel(tc, x, gamma, beta, norm, y, grad_out, out):
                 make_x_over_norm(0, (n,))
             make_dn(0)
             load_norm_grad_x(2)
+            new_result(0)
             load_y(0)
             gamma_rows_0 = load_gamma(0)
             gamma_rows_1 = load_gamma(1)
@@ -288,8 +291,12 @@ def tile_gdn_t_v_kernel(tc, x, gamma, beta, norm, y, grad_out, out):
             quantise_dn(0)
             make_x_over_norm(1)
             make_dn(1)
+            new_result(1)
             load_y(1)
             load_norm_grad_x(3)
+            new_result(2)
+            new_result(3)
+            load_y(3)
             load_y(2)
             new_roots(2)
             new_unit(2)
@@ -316,7 +323,6 @@ def tile_gdn_t_v_kernel(tc, x, gamma, beta, norm, y, grad_out, out):
             quantise_gamma(1, 1, grouped)
             make_factor(nc.vector, 0, 3 * N_TILE, 4 * N_TILE)
             load_norm_grad_x(4)
-            load_y(3)
             multiply(0, range(PACK), usual)
             new_roots(3)
             inverse_root(3)
@@ -326,10 +332,11 @@ def tile_gdn_t_v_kernel(tc, x, gamma, beta, norm, y, grad_out, out):
 
             for i in range(LAG, UNITS):
                 u = i - LAG
+                if i + 1 < UNITS:
+                    new_result(i + 1)
+                    load_y(i + 1)
                 if i + 2 < UNITS:
                     load_norm_grad_x(i + 2)
-                if i + 1 < UNITS:
-                    load_y(i + 1)
                 new_unit(i)
                 if i > LAG:
                     root(i)

@@ -140,9 +140,11 @@ def tile_gdn_t_v_kernel(tc, x, gamma, beta, norm, y, grad_out, out):
                 nc.tensor.transpose(bank[:, k, :], turned[:, k, :], identity_words[:])
             return bank
 
-        def stage_grad(u):
+        def turn_grad(u):
             words = flat(raw[u][1][:]).bitcast(F32)
-            banks = [turn(psum_x, words, n * N_TILE) for n in range(len(HALVES))]
+            return [turn(psum_x, words, n * N_TILE) for n in range(len(HALVES))]
+
+        def turn_grad_back(u, banks):
             grad_banks[u] = [turn_back(copy_turned(bank)) for bank in banks]
 
         def x_to_psum(u):
@@ -301,7 +303,7 @@ def tile_gdn_t_v_kernel(tc, x, gamma, beta, norm, y, grad_out, out):
             new_roots(2)
             new_unit(2)
             inverse_root(2)
-            stage_grad(2)
+            turn_grad_back(2, turn_grad(2))
             x_to_psum(2)
             root(0)
             inverse_norm(2)
@@ -326,7 +328,7 @@ def tile_gdn_t_v_kernel(tc, x, gamma, beta, norm, y, grad_out, out):
             multiply(0, range(PACK), usual)
             new_roots(3)
             inverse_root(3)
-            stage_grad(3)
+            turn_grad_back(3, turn_grad(3))
             inverse_norm(3)
             x_to_psum(3)
 
@@ -343,12 +345,12 @@ def tile_gdn_t_v_kernel(tc, x, gamma, beta, norm, y, grad_out, out):
                 second_term(u, range(PACK))
                 y_words = flat(raw[i][3][:])
                 turned = [turn(psum_m, y_words, t * N_TILE) for t in (2, 3)]
-                multiply(u + 1, range(2), usual)
+                multiply(u + 1, (0,), usual)
                 make_first_term(i)
                 y_banks = [turn_back(copy_turned(bank)) for bank in turned]
                 if i == LAG:
                     root(i)
-                multiply(u + 1, range(2, PACK), usual)
+                multiply(u + 1, (1, 2), usual)
                 make_x_over_norm(i)
                 for n in range(2):
                     make_factor_from_psum(i, 2 + n, y_banks[n])
@@ -357,9 +359,13 @@ def tile_gdn_t_v_kernel(tc, x, gamma, beta, norm, y, grad_out, out):
                 if i + 1 < UNITS:
                     new_roots(i + 1)
                     inverse_root(i + 1)
-                    stage_grad(i + 1)
+                    turned = turn_grad(i + 1)
+                    multiply(u + 1, (3,), usual)
+                    turn_grad_back(i + 1, turned)
                     inverse_norm(i + 1)
                     x_to_psum(i + 1)
+                else:
+                    multiply(u + 1, (3,), usual)
                 for s in thirds:
                     add_terms(nc.gpsimd, u, s)
                 make_factor(nc.gpsimd, i, 0, 3 * N_TILE // 2)

@@ -54,7 +54,7 @@ def tile_gdn_t_v_kernel(tc, x, gamma, beta, norm, y, grad_out, out):
 
     with ExitStack() as stack:
         keep = stack.enter_context(tc.tile_pool(name="keep", bufs=1))
-        stage = stack.enter_context(tc.tile_pool(name="stage", bufs=PASSES))
+        stage = stack.enter_context(tc.tile_pool(name="stage", bufs=2 * PASSES))
         grouping = stack.enter_context(tc.tile_pool(name="grouping", bufs=3))
         loads = stack.enter_context(tc.tile_pool(name="loads", bufs=AHEAD))
         short = stack.enter_context(tc.tile_pool(name="short", bufs=2))
@@ -83,16 +83,31 @@ def tile_gdn_t_v_kernel(tc, x, gamma, beta, norm, y, grad_out, out):
         def pieces(u, h):
             return QUARTERS[h] if u == 0 and h == HALVES[0] else (h,)
 
-        def load_norm_grad_x(u):
+        def new_inputs(u):
             norm_t = loads.tile([P, PACK, N_TILE], F32)
             grad_t = loads.tile([P, PACK, N_TILE], BF16)
             x_t = loads.tile([P, PACK, N_TILE], BF16)
-            for h in HALVES:
-                for s in pieces(u, h):
-                    nc.sync.dma_start(out=norm_t[:, s, :], in_=dram_unit(norm_units, u)[:, s, :])
-                    nc.sync.dma_start(out=grad_t[:, s, :], in_=dram_unit(grad_units, u)[:, s, :])
-                nc.sync.dma_start(out=x_t[:, h, :], in_=dram_unit(x_units, u)[:, h, :])
             raw[u] = [norm_t, grad_t, x_t]
+
+        def load_norm(u, s):
+            nc.sync.dma_start(out=raw[u][0][:, s, :], in_=dram_unit(norm_units, u)[:, s, :])
+
+        def load_grad(u, s):
+            nc.sync.dma_start(out=raw[u][1][:, s, :], in_=dram_unit(grad_units, u)[:, s, :])
+
+        def load_norm_grad(u):
+            new_inputs(u)
+            for h in HALVES:
+                load_norm(u, h)
+                load_grad(u, h)
+
+        def load_x(u, h):
+            nc.sync.dma_start(out=raw[u][2][:, h, :], in_=dram_unit(x_units, u)[:, h, :])
+
+        def load_norm_grad_x(u):
+            load_norm_grad(u)
+            for h in HALVES:
+                load_x(u, h)
 
         def new_result(u):
             result = results.tile([P, PACK, N_TILE], F32)
@@ -156,17 +171,16 @@ def tile_gdn_t_v_kernel(tc, x, gamma, beta, norm, y, grad_out, out):
                     nc.tensor.matmul(out=bank[:, j, :], lhsT=identity[:], rhs=x_t[:, h.start + j, :], start=True, stop=True)
                 x_banks[u].append(bank)
 
-        def load_gamma(g):
-            gamma_rows = stage.tile([P, PACK, CHANNELS], BF16)
-            nc.sync.dma_start(out=gamma_rows[:], in_=gamma_passes[g])
+        def load_gamma(g, part):
+            gamma_rows = stage.tile([P, PACK, N_TILE], BF16)
+            nc.sync.dma_start(out=gamma_rows[:], in_=gamma_passes[g, :, :, part * N_TILE : (part + 1) * N_TILE])
             return gamma_rows
 
-        def regroup_gamma(gamma_rows, part):
-            c = slice(part * N_TILE, (part + 1) * N_TILE)
+        def regroup_gamma(gamma_rows):
             gamma_grouped = grouping.tile([P, N_TILE, PACK], BF16, align_bytes=64)
             nc.scalar.copy(
                 out=gamma_grouped[:].rearrange("p (c i) t -> p c t i", i=4),
-                in_=gamma_rows[:, :, c].rearrange("p t (c i) -> p c t i", i=4),
+                in_=gamma_rows[:].rearrange("p t (c i) -> p c t i", i=4),
             )
             return gamma_grouped
 
@@ -270,8 +284,22 @@ def tile_gdn_t_v_kernel(tc, x, gamma, beta, norm, y, grad_out, out):
             slot = [slice(t, t + 1) for t in range(PACK)]
             thirds = (slot[0], slice(1, PACK - 1), slot[PACK - 1])
             usual = [psum_m] * PACK
-            load_norm_grad_x(0)
-            load_norm_grad_x(1)
+            new_inputs(0)
+            new_inputs(1)
+            low, high = HALVES
+            for s in QUARTERS[low]:
+                load_norm(0, s)
+                load_grad(0, s)
+            load_norm(0, high)
+            load_x(0, low)
+            load_grad(0, high)
+            load_norm(1, low)
+            load_x(0, high)
+            load_norm(1, high)
+            load_grad(1, low)
+            load_grad(1, high)
+            load_x(1, low)
+            load_x(1, high)
             new_roots(0)
             new_unit(0)
             for n in range(len(HALVES)):
@@ -280,11 +308,16 @@ def tile_gdn_t_v_kernel(tc, x, gamma, beta, norm, y, grad_out, out):
                 make_first_term(0, (n,))
                 make_x_over_norm(0, (n,))
             make_dn(0)
-            load_norm_grad_x(2)
+            new_inputs(2)
+            load_norm(2, low)
+            load_norm(2, high)
+            load_grad(2, low)
+            load_grad(2, high)
             new_result(0)
             load_y(0)
-            gamma_rows_0 = load_gamma(0)
-            gamma_rows_1 = load_gamma(1)
+            load_x(2, low)
+            load_x(2, high)
+            gamma_rows = [load_gamma(g, 0) for g in range(PASSES)]
             new_roots(1)
             new_unit(1)
             inverse_root(1)
@@ -299,6 +332,7 @@ def tile_gdn_t_v_kernel(tc, x, gamma, beta, norm, y, grad_out, out):
             new_result(2)
             new_result(3)
             load_y(3)
+            late_gamma_rows = [load_gamma(g, 1) for g in range(PASSES)]
             load_y(2)
             new_roots(2)
             new_unit(2)
@@ -311,24 +345,22 @@ def tile_gdn_t_v_kernel(tc, x, gamma, beta, norm, y, grad_out, out):
             make_x_over_norm(2)
             make_factor(nc.gpsimd, 0, 0, 3 * N_TILE)
             quantise_dn(1)
-            grouped = regroup_gamma(gamma_rows_0, 0)
+            grouped = regroup_gamma(gamma_rows[0])
             quantise_gamma(0, 0, grouped)
             make_dn(2)
-            grouped = regroup_gamma(gamma_rows_0, 1)
-            quantise_gamma(0, 1, grouped)
-            grouped = regroup_gamma(gamma_rows_1, 0)
-            quantise_dn(2)
+            grouped = regroup_gamma(gamma_rows[1])
             quantise_gamma(1, 0, grouped)
+            quantise_dn(2)
             root(1)
-            make_factor(nc.vector, 1, 0, 4 * N_TILE)
-            grouped = regroup_gamma(gamma_rows_1, 1)
-            quantise_gamma(1, 1, grouped)
+            make_factor(nc.vector, 1, 0, 2 * N_TILE)
+            make_factor(nc.vector, 1, 2 * N_TILE, 4 * N_TILE)
             make_factor(nc.vector, 0, 3 * N_TILE, 4 * N_TILE)
             load_norm_grad_x(4)
-            multiply(0, range(PACK), usual)
             new_roots(3)
             inverse_root(3)
-            turn_grad_back(3, turn_grad(3))
+            turned = turn_grad(3)
+            multiply(0, range(PACK), usual)
+            turn_grad_back(3, turned)
             inverse_norm(3)
             x_to_psum(3)
 
@@ -345,18 +377,21 @@ def tile_gdn_t_v_kernel(tc, x, gamma, beta, norm, y, grad_out, out):
                 second_term(u, range(PACK))
                 y_words = flat(raw[i][3][:])
                 turned = [turn(psum_m, y_words, t * N_TILE) for t in (2, 3)]
-                multiply(u + 1, (0,), usual)
+                if i > LAG:
+                    multiply(u + 1, (0,), usual)
                 make_first_term(i)
                 y_banks = [turn_back(copy_turned(bank)) for bank in turned]
                 if i == LAG:
                     root(i)
-                multiply(u + 1, (1, 2), usual)
+                if i > LAG:
+                    multiply(u + 1, (1, 2), usual)
                 make_x_over_norm(i)
                 for n in range(2):
                     make_factor_from_psum(i, 2 + n, y_banks[n])
                 if i == LAG:
+                    late_gamma = [regroup_gamma(rows) for rows in late_gamma_rows]
                     root(i - 1)
-                if i + 1 < UNITS:
+                if LAG < i < UNITS - 1:
                     new_roots(i + 1)
                     inverse_root(i + 1)
                     turned = turn_grad(i + 1)
@@ -364,16 +399,27 @@ def tile_gdn_t_v_kernel(tc, x, gamma, beta, norm, y, grad_out, out):
                     turn_grad_back(i + 1, turned)
                     inverse_norm(i + 1)
                     x_to_psum(i + 1)
-                else:
+                elif i > LAG:
                     multiply(u + 1, (3,), usual)
                 for s in thirds:
                     add_terms(nc.gpsimd, u, s)
-                make_factor(nc.gpsimd, i, 0, 3 * N_TILE // 2)
+                make_factor(nc.gpsimd, i, 0, 7 * N_TILE // 4)
                 make_dn(i)
-                make_factor(nc.vector, i, 3 * N_TILE // 2, 2 * N_TILE)
+                make_factor(nc.vector, i, 7 * N_TILE // 4, 2 * N_TILE)
                 quantise_dn(i)
                 if i == LAG:
-                    make_factor(nc.vector, i - 1, 0, 4 * N_TILE)
+                    for g in range(PASSES):
+                        quantise_gamma(g, 1, late_gamma[g])
+                    make_factor(nc.vector, i - 1, 0, 2 * N_TILE)
+                    make_factor(nc.vector, i - 1, 2 * N_TILE, 4 * N_TILE)
+                    multiply(u + 1, (0, 1), usual)
+                    new_roots(i + 1)
+                    inverse_root(i + 1)
+                    turned = turn_grad(i + 1)
+                    multiply(u + 1, (2, 3), usual)
+                    turn_grad_back(i + 1, turned)
+                    inverse_norm(i + 1)
+                    x_to_psum(i + 1)
                 for h in HALVES:
                     store(u, h)
 

from contextlib import ExitStack

import concourse.mybir as mybir
from concourse.masks import make_identity

F32 = mybir.dt.float32
BF16 = mybir.dt.bfloat16
U32 = mybir.dt.uint32
U8 = mybir.dt.uint8
E4M3_X4 = mybir.dt.float8_e4m3fn_x4
E5M2_X4 = mybir.dt.float8_e5m2_x4
ACT = mybir.ActivationFunctionType
ALU = mybir.AluOpType

BATCH = 2
CHANNELS = 1024
PIXELS = 32 * 32
P = 128
PACK = 4
K_PASS = P * PACK
PASSES = CHANNELS // K_PASS
N_TILE = 512
BLOCKS = BATCH * PIXELS // N_TILE
UNITS = BLOCKS * PASSES
LAG = 3
AHEAD = 2
HALVES = (slice(0, PACK // 2), slice(PACK // 2, PACK))
QUARTERS = tuple(slice(t, t + 1) for t in range(PACK))

FLOPS = 2 * BATCH * PIXELS * CHANNELS * CHANNELS


def flat(ap):
    return ap.rearrange("p t w -> p (t w)")


def tile_gdn_t_v_kernel(tc, x, gamma, beta, norm, y, grad_out, out):
    nc = tc.nc

    def units_of(ap):
        return ap.rearrange("b (g t p) h w -> b g p t (h w)", t=PACK, p=P)

    x_units = units_of(x)
    norm_units = units_of(norm)
    y_units = units_of(y)
    grad_units = units_of(grad_out)
    out_units = units_of(out)
    gamma_passes = gamma.rearrange("(g t p) c -> g p t c", t=PACK, p=P)

    def dram_unit(units, u):
        block, g = divmod(u, PASSES)
        b, part = divmod(block, PIXELS // N_TILE)
        return units[b, g, :, :, part * N_TILE : (part + 1) * N_TILE]

    with ExitStack() as stack:
        keep = stack.enter_context(tc.tile_pool(name="keep", bufs=1))
        stage = stack.enter_context(tc.tile_pool(name="stage", bufs=2 * PASSES))
        grouping = stack.enter_context(tc.tile_pool(name="grouping", bufs=3))
        loads = stack.enter_context(tc.tile_pool(name="loads", bufs=AHEAD))
        short = stack.enter_context(tc.tile_pool(name="short", bufs=2))
        once = stack.enter_context(tc.tile_pool(name="once", bufs=1))
        kept = stack.enter_context(tc.tile_pool(name="kept", bufs=LAG + 2))
        results = stack.enter_context(tc.tile_pool(name="results", bufs=LAG + 2))
        coded = stack.enter_context(tc.tile_pool(name="coded", bufs=LAG + 3))
        psum_m = stack.enter_context(tc.psum_pool(name="psum_m", bufs=PACK))
        psum_x = stack.enter_context(tc.psum_pool(name="psum_x", bufs=len(HALVES)))
        psum_g = stack.enter_context(tc.psum_pool(name="psum_g", bufs=len(HALVES)))

        gamma_codes = keep.tile([P, PASSES, CHANNELS], U32, align_bytes=64)
        gamma_scales = keep.tile([P, PASSES, CHANNELS], U8, align_bytes=64)
        identity = keep.tile([P, P], BF16)
        make_identity(nc, identity[:])
        identity_words = keep.tile([P, P], F32)
        make_identity(nc, identity_words[:])

        raw = {}
        roots = {}
        x_banks = {}
        grad_banks = {}
        made = {}
        sums = {}

        def pieces(u, h):
            return QUARTERS[h] if u == 0 and h == HALVES[0] else (h,)

        def new_inputs(u):
            norm_t = loads.tile([P, PACK, N_TILE], F32)
            grad_t = loads.tile([P, PACK, N_TILE], BF16)
            x_t = loads.tile([P, PACK, N_TILE], BF16)
            raw[u] = [norm_t, grad_t, x_t]

        def load_norm(u, s):
            nc.sync.dma_start(out=raw[u][0][:, s, :], in_=dram_unit(norm_units, u)[:, s, :])

        def load_grad(u, s):
            nc.sync.dma_start(out=raw[u][1][:, s, :], in_=dram_unit(grad_units, u)[:, s, :])

        def load_norm_grad(u):
            new_inputs(u)
            for h in HALVES:
                load_norm(u, h)
                load_grad(u, h)

        def load_x(u, h):
            nc.sync.dma_start(out=raw[u][2][:, h, :], in_=dram_unit(x_units, u)[:, h, :])

        def load_norm_grad_x(u):
            load_norm_grad(u)
            for h in HALVES:
                load_x(u, h)

        def new_result(u):
            result = results.tile([P, PACK, N_TILE], F32)
            raw[u].append(result)

        def load_y(u):
            nc.sync.dma_start(out=raw[u][3][:], in_=dram_unit(y_units, u))

        def new_roots(u):
            inv_root = short.tile([P, PACK, N_TILE], F32)
            inv_norm = short.tile([P, PACK, N_TILE], F32)
            roots[u] = [inv_root, inv_norm]

        def inverse_root(u, halves=HALVES):
            for h in halves:
                for s in pieces(u, h):
                    nc.scalar.activation(out=roots[u][0][:, s, :], in_=raw[u][0][:, s, :], func=ACT.Abs_reciprocal_sqrt)

        def inverse_norm(u, halves=HALVES):
            for h in halves:
                nc.scalar.activation(out=roots[u][1][:, h, :], in_=roots[u][0][:, h, :], func=ACT.Square)

        def root(u):
            inv_norm = roots[u][1]
            root_t = short.tile([P, PACK, N_TILE], F32)
            for h in HALVES:
                nc.scalar.activation(out=root_t[:, h, :], in_=inv_norm[:, h, :], func=ACT.Abs_reciprocal_sqrt)
            roots[u].append(root_t)

        def turn(pool, words, first_word):
            turned_bank = pool.tile([P, PACK, P], F32, tag="bank")
            for k in range(PACK):
                w0 = first_word + k * P
                nc.tensor.transpose(turned_bank[:, k, :], words[:, w0 : w0 + P], identity_words[:])
            return turned_bank

        def copy_turned(turned_bank):
            turned = short.tile([P, PACK, P], F32)
            nc.scalar.copy(out=turned[:], in_=turned_bank[:])
            return turned

        def turn_back(turned):
            bank = psum_g.tile([P, PACK, P], F32, tag="bank")
            for k in range(PACK):
                nc.tensor.transpose(bank[:, k, :], turned[:, k, :], identity_words[:])
            return bank

        def turn_grad(u):
            words = flat(raw[u][1][:]).bitcast(F32)
            return [turn(psum_x, words, n * N_TILE) for n in range(len(HALVES))]

        def turn_grad_back(u, banks):
            grad_banks[u] = [turn_back(copy_turned(bank)) for bank in banks]

        def x_to_psum(u):
            x_t = raw[u][2]
            x_banks[u] = []
            for h in HALVES:
                bank = psum_x.tile([P, PACK // 2, N_TILE], BF16, tag="bank")
                for j in range(PACK // 2):
                    nc.tensor.matmul(out=bank[:, j, :], lhsT=identity[:], rhs=x_t[:, h.start + j, :], start=True, stop=True)
                x_banks[u].append(bank)

        def load_gamma(g, part):
            gamma_rows = stage.tile([P, PACK, N_TILE], BF16)
            nc.sync.dma_start(out=gamma_rows[:], in_=gamma_passes[g, :, :, part * N_TILE : (part + 1) * N_TILE])
            return gamma_rows

        def regroup_gamma(gamma_rows):
            gamma_grouped = grouping.tile([P, N_TILE, PACK], BF16, align_bytes=64)
            nc.scalar.copy(
                out=gamma_grouped[:].rearrange("p (c i) t -> p c t i", i=4),
                in_=gamma_rows[:].rearrange("p t (c i) -> p c t i", i=4),
            )
            return gamma_grouped

        def quantise_gamma(g, part, gamma_grouped):
            c = slice(part * N_TILE, (part + 1) * N_TILE)
            nc.vector.quantize_mx(
                out=gamma_codes[:, g, c].bitcast(E4M3_X4),
                scales=gamma_scales[:, g, c],
                in_=gamma_grouped[:].rearrange("p c t -> p (c t)"),
            )

        def new_unit(u):
            first = kept.tile([P, PACK, N_TILE], F32)
            x_over_norm = once.tile([P, PACK, N_TILE], F32)
            made[u] = [first, x_over_norm]

        def make_first_term(u, halves=(0, 1)):
            for n in halves:
                for s in pieces(u, HALVES[n]):
                    if u in grad_banks:
                        grad_part = grad_banks[u][n][:].rearrange("p k w -> p (k w)").bitcast(BF16)
                    else:
                        grad_part = flat(raw[u][1][:, s, :])
                    nc.vector.tensor_tensor(
                        out=flat(made[u][0][:, s, :]), in0=grad_part, in1=flat(roots[u][0][:, s, :]), op=ALU.mult,
                    )

        def make_x_over_norm(u, halves=(0, 1)):
            for n in halves:
                h = HALVES[n]
                x_half = x_banks[u][n][:] if u in x_banks else raw[u][2][:, h, :]
                nc.vector.scalar_tensor_tensor(
                    out=flat(made[u][1][:, h, :]), in0=flat(x_half), scalar=-0.5, in1=flat(roots[u][1][:, h, :]),
                    op0=ALU.mult, op1=ALU.mult,
                )

        def make_dn(u):
            first, x_over_norm = made[u]
            dn_grouped = short.tile([P, N_TILE, PACK], BF16, align_bytes=64)
            nc.vector.tensor_tensor(
                out=dn_grouped[:].rearrange("p (c i) t -> p c t i", i=4),
                in0=first[:].rearrange("p t (c i) -> p c t i", i=4),
                in1=x_over_norm[:].rearrange("p t (c i) -> p c t i", i=4),
                op=ALU.mult,
            )
            made[u].append(dn_grouped)

        def quantise_dn(u):
            dn_codes = coded.tile([P, N_TILE], U32, align_bytes=64)
            dn_scales = coded.tile([P, N_TILE], U8, align_bytes=64)
            nc.vector.quantize_mx(
                out=dn_codes[:].bitcast(E5M2_X4),
                scales=dn_scales[:],
                in_=made[u][2][:].rearrange("p w t -> p (w t)"),
            )
            made[u].append((dn_codes, dn_scales))

        def make_factor(engine, u, first_column, end_column):
            w = slice(first_column, end_column)
            result = flat(raw[u][3][:])
            engine.tensor_tensor(out=result[:, w], in0=result[:, w], in1=flat(roots[u][2][:])[:, w], op=ALU.mult)

        def make_factor_from_psum(u, t, bank):
            nc.vector.tensor_tensor(
                out=raw[u][3][:, t, :], in0=bank[:].rearrange("p k w -> p (k w)"), in1=roots[u][2][:, t, :], op=ALU.mult,
            )

        def multiply(u, slots, pools):
            block, g_out = divmod(u, PASSES)
            for t in slots:
                c0 = (g_out * PACK + t) * P
                m = pools[t].tile([P, N_TILE], F32, tag="bank")
                for g in range(PASSES):
                    dn_codes, dn_scales = made[block * PASSES + g][3]
                    nc.tensor.matmul_mx(
                        out=m[:],
                        lhsT=gamma_codes[:, g, c0 : c0 + P].bitcast(E4M3_X4),
                        lhsT_scale=gamma_scales[:, g, c0 : c0 + P],
                        rhs=dn_codes[:].bitcast(E5M2_X4),
                        rhs_scale=dn_scales[:],
                        start=(g == 0),
                        stop=(g == PASSES - 1),
                    )
                sums.setdefault(u, []).append(m)

        def second_term(u, slots):
            result = raw[u][3]
            for t in slots:
                nc.vector.scalar_tensor_tensor(
                    out=result[:, t, :], in0=sums[u][t][:], scalar=2.0, in1=result[:, t, :], op0=ALU.mult, op1=ALU.mult,
                )

        def add_terms(engine, u, s):
            result = raw[u][3]
            engine.tensor_tensor(out=flat(result[:, s, :]), in0=flat(result[:, s, :]), in1=flat(made[u][0][:, s, :]), op=ALU.add)

        def store(u, s):
            nc.sync.dma_start(out=dram_unit(out_units, u)[:, s, :], in_=raw[u][3][:, s, :])

        with tc.manual_schedule():
            slot = [slice(t, t + 1) for t in range(PACK)]
            thirds = (slot[0], slice(1, PACK - 1), slot[PACK - 1])
            usual = [psum_m] * PACK
            new_inputs(0)
            new_inputs(1)
            low, high = HALVES
            for s in QUARTERS[low]:
                load_norm(0, s)
                load_grad(0, s)
            load_norm(0, high)
            load_x(0, low)
            load_grad(0, high)
            load_norm(1, low)
            load_x(0, high)
            load_norm(1, high)
            load_grad(1, low)
            load_grad(1, high)
            load_x(1, low)
            load_x(1, high)
            new_roots(0)
            new_unit(0)
            for n in range(len(HALVES)):
                inverse_root(0, HALVES[n : n + 1])
                inverse_norm(0, HALVES[n : n + 1])
                make_first_term(0, (n,))
                make_x_over_norm(0, (n,))
            make_dn(0)
            new_inputs(2)
            load_norm(2, low)
            load_norm(2, high)
            load_grad(2, low)
            load_grad(2, high)
            new_result(0)
            load_y(0)
            load_x(2, low)
            load_x(2, high)
            gamma_rows = [load_gamma(g, 0) for g in range(PASSES)]
            new_roots(1)
            new_unit(1)
            inverse_root(1)
            inverse_norm(1)
            make_first_term(1)
            quantise_dn(0)
            make_x_over_norm(1)
            make_dn(1)
            new_result(1)
            load_y(1)
            load_norm_grad_x(3)
            new_result(2)
            new_result(3)
            load_y(3)
            late_gamma_rows = [load_gamma(g, 1) for g in range(PASSES)]
            load_y(2)
            new_roots(2)
            new_unit(2)
            inverse_root(2)
            turn_grad_back(2, turn_grad(2))
            x_to_psum(2)
            root(0)
            inverse_norm(2)
            make_first_term(2)
            make_x_over_norm(2)
            make_factor(nc.gpsimd, 0, 0, 3 * N_TILE)
            quantise_dn(1)
            grouped = regroup_gamma(gamma_rows[0])
            quantise_gamma(0, 0, grouped)
            make_dn(2)
            grouped = regroup_gamma(gamma_rows[1])
            quantise_gamma(1, 0, grouped)
            quantise_dn(2)
            root(1)
            make_factor(nc.vector, 1, 0, 2 * N_TILE)
            make_factor(nc.vector, 1, 2 * N_TILE, 4 * N_TILE)
            make_factor(nc.vector, 0, 3 * N_TILE, 4 * N_TILE)
            load_norm_grad_x(4)
            new_roots(3)
            inverse_root(3)
            turned = turn_grad(3)
            multiply(0, range(PACK), usual)
            turn_grad_back(3, turned)
            inverse_norm(3)
            x_to_psum(3)

            for i in range(LAG, UNITS):
                u = i - LAG
                if i + 1 < UNITS:
                    new_result(i + 1)
                    load_y(i + 1)
                if i + 2 < UNITS:
                    load_norm_grad_x(i + 2)
                new_unit(i)
                if i > LAG:
                    root(i)
                second_term(u, range(PACK))
                y_words = flat(raw[i][3][:])
                turned = [turn(psum_m, y_words, t * N_TILE) for t in (2, 3)]
                if i > LAG:
                    multiply(u + 1, (0,), usual)
                make_first_term(i)
                y_banks = [turn_back(copy_turned(bank)) for bank in turned]
                if i == LAG:
                    root(i)
                if i > LAG:
                    multiply(u + 1, (1, 2), usual)
                make_x_over_norm(i)
                for n in range(2):
                    make_factor_from_psum(i, 2 + n, y_banks[n])
                if i == LAG:
                    late_gamma = [regroup_gamma(rows) for rows in late_gamma_rows]
                    root(i - 1)
                if LAG < i < UNITS - 1:
                    new_roots(i + 1)
                    inverse_root(i + 1)
                    turned = turn_grad(i + 1)
                    multiply(u + 1, (3,), usual)
                    turn_grad_back(i + 1, turned)
                    inverse_norm(i + 1)
                    x_to_psum(i + 1)
                elif i > LAG:
                    multiply(u + 1, (3,), usual)
                for s in thirds:
                    add_terms(nc.gpsimd, u, s)
                make_factor(nc.gpsimd, i, 0, 7 * N_TILE // 4)
                make_dn(i)
                make_factor(nc.vector, i, 7 * N_TILE // 4, 2 * N_TILE)
                quantise_dn(i)
                if i == LAG:
                    for g in range(PASSES):
                        quantise_gamma(g, 1, late_gamma[g])
                    make_factor(nc.vector, i - 1, 0, 2 * N_TILE)
                    make_factor(nc.vector, i - 1, 2 * N_TILE, 4 * N_TILE)
                    multiply(u + 1, (0, 1), usual)
                    new_roots(i + 1)
                    inverse_root(i + 1)
                    turned = turn_grad(i + 1)
                    multiply(u + 1, (2, 3), usual)
                    turn_grad_back(i + 1, turned)
                    inverse_norm(i + 1)
                    x_to_psum(i + 1)
                for h in HALVES:
                    store(u, h)

            a, b, c = UNITS - 3, UNITS - 2, UNITS - 1
            second_term(a, range(PACK))
            multiply(b, range(PACK), [psum_x, psum_x, psum_g, psum_g])
            multiply(c, range(PACK), usual)
            second_term(b, range(PACK))
            second_term(c, range(PACK))
            for s in thirds:
                add_terms(nc.gpsimd, a, s)
            add_terms(nc.gpsimd, b, slot[0])
            for h in HALVES:
                store(a, h)
            add_terms(nc.vector, c, slot[PACK - 1])
            add_terms(nc.vector, b, slot[1])
            store(c, slot[PACK - 1])
            store(b, HALVES[0])
            add_terms(nc.vector, b, HALVES[1])
            store(b, HALVES[1])
            for t in range(PACK - 1):
                add_terms(nc.vector, c, slot[t])
                store(c, slot[t])
